import numpy as np
import ml_dtypes


def mxq(x, axis, fmt="e4m3"):
    dtype, down = {"e4m3": (ml_dtypes.float8_e4m3fn, 7), "e5m2": (ml_dtypes.float8_e5m2, 14)}[fmt]
    v = np.moveaxis(np.asarray(x, np.float32).astype(ml_dtypes.bfloat16).astype(np.float64), axis, -1)
    blocks = v.reshape(v.shape[:-1] + (-1, 32))
    amax = np.abs(blocks).max(-1, keepdims=True)
    byte = np.maximum(np.where(amax > 0, np.frexp(amax)[1] - 1 + 127, 0) - down, 1)
    scale = np.exp2(byte - 127.0)
    codes = (blocks / scale).astype(np.float32).astype(dtype).astype(np.float64)
    return np.moveaxis((codes * scale).reshape(v.shape), -1, axis)


WIDE = False


def mx_kscale(k):
    if not WIDE:
        return np.ones(k)
    levels = np.array([10, -10, 5, -5, 0])
    a = np.random.permutation(np.resize(levels, k // 512 * 4)).reshape(k // 512, 4)
    idx = np.arange(k)
    return np.exp2(a[idx // 512, idx % 128 // 32])


BF16 = ml_dtypes.bfloat16


def bf(x):
    return np.asarray(x, np.float32).astype(BF16)


def f64(x):
    return np.asarray(x).astype(np.float64)


N, C, D, H, W, NHEADS, KSIZE = 1, 1024, 256, 16, 16, 8, 5
PAD = KSIZE // 2
HD = D // NHEADS
WIN = KSIZE * KSIZE


def _patches(t):
    tp = np.pad(t, ((0, 0), (0, 0), (PAD, PAD), (PAD, PAD)))
    return np.stack([tp[:, :, i:i + H, j:j + W] for i in range(KSIZE) for j in range(KSIZE)], axis=2)


def setup_inputs():
    s = mx_kscale(C)
    a = np.sqrt(1.5) / HD ** 0.25
    g = np.concatenate([np.full(2 * D, a), np.ones(D)])
    return {"x": bf(np.random.standard_normal((N, C, H, W)) * s[None, :, None, None]),
            "w_qkv": bf(np.random.standard_normal((3 * D, C)) * g[:, None] / np.sqrt(C) / s[None, :])}


def reference(x, w_qkv):
    xq = mxq(f64(x).reshape(N, C, H * W), 1, "e4m3")
    wq = mxq(f64(w_qkv), 1, "e4m3")
    qkv = (wq @ xq).reshape(N, 3 * D, H, W)
    Q, K, V = np.split(qkv, 3, axis=1)
    Qh = Q.reshape(N, NHEADS, HD, 1, H, W)
    scores = np.sum(_patches(K).reshape(N, NHEADS, HD, WIN, H, W) * Qh, axis=2, keepdims=True)
    e = np.exp(scores - scores.max(axis=3, keepdims=True))
    att = e / e.sum(axis=3, keepdims=True)
    out = np.sum(_patches(V).reshape(N, NHEADS, HD, WIN, H, W) * att, axis=3).reshape(N, D, H, W)
    return out

@@ -1,0 +1,242 @@
+from contextlib import ExitStack
+
+import concourse.mybir as mybir
+from concourse.masks import make_identity
+
+F32 = mybir.dt.float32
+BF16 = mybir.dt.bfloat16
+U32 = mybir.dt.uint32
+U8 = mybir.dt.uint8
+FP8X4 = mybir.dt.float8_e4m3fn_x4
+ALU = mybir.AluOpType
+ACT = mybir.ActivationFunctionType
+AXIS_X = mybir.AxisListType.X
+
+P = 128
+PACK = 4
+C_IN = 1024
+PASSES = C_IN // (P * PACK)
+D = 256
+HEADS = 8
+HEAD_DIM = D // HEADS
+SIDE = 16
+PIX = SIDE * SIDE
+KSIZE = 5
+PAD = KSIZE // 2
+WIN = KSIZE * KSIZE
+PIX_TILES = PIX // P
+ROWS = P // SIDE
+CH_TILES = D // P
+FULL_OFFSETS = P // HEADS
+
+FLOPS = 2 * 3 * D * C_IN * PIX + 2 * 2 * D * WIN * PIX
+
+
+def tile_relation_s_kernel(tc, x, w_qkv, out):
+    nc = tc.nc
+    with ExitStack() as ctx:
+        keep = ctx.enter_context(tc.tile_pool(name="keep", bufs=1))
+        small = ctx.enter_context(tc.tile_pool(name="small", bufs=2))
+        work = ctx.enter_context(tc.tile_pool(name="work", bufs=4))
+        stream = ctx.enter_context(tc.psum_pool(name="stream", bufs=4))
+        sums = ctx.enter_context(tc.psum_pool(name="sums", bufs=4))
+
+        x_sb = keep.tile([P, PASSES, PACK, PIX], BF16)
+        nc.sync.dma_start(
+            out=x_sb[:].rearrange("p g (u e) w -> p (g u) (e w)", u=2, e=2),
+            in_=x.rearrange("n (a q e) h w -> q (n a) (e h w)", a=PASSES * 2, q=P, e=2),
+        )
+        first_row = {"q": 0, "k": D, "v": 2 * D}
+        w_sb = {}
+        for part in ("k", "q", "v"):
+            w_sb[part] = keep.tile([P, CH_TILES, C_IN], BF16, name="w_sb_" + part)
+            rows = w_qkv[first_row[part] : first_row[part] + D, :]
+            nc.sync.dma_start(out=w_sb[part][:], in_=rows.rearrange("(a p) k -> p a k", p=P))
+
+        ident = keep.tile([P, P], F32)
+        make_identity(nc, ident[:])
+        k_shift = keep.tile([P, KSIZE, CH_TILES, SIDE + 2 * PAD, SIDE], F32)
+        v_shift = keep.tile([P, KSIZE, CH_TILES, SIDE + 2 * PAD, SIDE], F32)
+        nc.vector.memset(k_shift[:], 0.0)
+        nc.vector.memset(v_shift[:], 0.0)
+        warm = keep.tile([P, 1], F32)
+        nc.vector.memset(warm[:], 0.0)
+        warm_out = keep.tile([P, 1], F32)
+        nc.scalar.activation(out=warm_out[:], in_=warm[:], func=ACT.Exp)
+
+        x_grouped = keep.tile([P, PASSES, PIX, PACK], BF16, align_bytes=64)
+        nc.vector.tensor_copy(out=x_grouped[:], in_=x_sb[:].rearrange("p g t w -> p g w t"))
+        x_codes = keep.tile([P, PASSES, PIX], U32, align_bytes=64)
+        x_scales = keep.tile([P, PASSES, PIX], U8, align_bytes=64)
+        nc.vector.quantize_mx(
+            out=x_codes[:].rearrange("p g w -> p (g w)").bitcast(FP8X4),
+            scales=x_scales[:].rearrange("p g w -> p (g w)"),
+            in_=x_grouped[:].rearrange("p g w t -> p (g w t)"),
+        )
+
+        w_codes = {}
+        w_scales = {}
+        for part in ("k", "q", "v"):
+            w_grouped = keep.tile([P, PASSES, D, PACK], BF16, align_bytes=64, name="w_grouped_" + part)
+            for ct in range(CH_TILES):
+                wt = stream.tile([P, PASSES * 2, P], F32, tag="stream")
+                words = w_sb[part][:, ct, :].bitcast(F32)
+                for gu in range(PASSES * 2):
+                    nc.tensor.transpose(wt[:, gu, :], words[:, gu * P : (gu + 1) * P], ident[:])
+                copy_out = nc.vector.tensor_copy if ct == 0 else nc.scalar.copy
+                copy_out(
+                    out=w_grouped[:].bitcast(F32)[:, :, ct * P : (ct + 1) * P, :],
+                    in_=wt[:].rearrange("p (g u) o -> p g o u", g=PASSES, u=2),
+                )
+            w_codes[part] = keep.tile([P, PASSES, D], U32, align_bytes=64, name="w_codes_" + part)
+            w_scales[part] = keep.tile([P, PASSES, D], U8, align_bytes=64, name="w_scales_" + part)
+            nc.vector.quantize_mx(
+                out=w_codes[part][:].rearrange("p g o -> p (g o)").bitcast(FP8X4),
+                scales=w_scales[part][:].rearrange("p g o -> p (g o)"),
+                in_=w_grouped[:].rearrange("p g o t -> p (g o t)"),
+            )
+
+        def project_channels_first(part, shifted, engines):
+            for ct in range(CH_TILES):
+                acc = sums.tile([P, PIX], F32, tag="sums")
+                cols = slice(ct * P, (ct + 1) * P)
+                for g in range(PASSES):
+                    nc.tensor.matmul_mx(
+                        out=acc[:],
+                        lhsT=w_codes[part][:, g, cols].bitcast(FP8X4),
+                        lhsT_scale=w_scales[part][:, g, cols],
+                        rhs=x_codes[:, g, :].bitcast(FP8X4),
+                        rhs_scale=x_scales[:, g, :],
+                        start=(g == 0),
+                        stop=(g == PASSES - 1),
+                    )
+                image = acc[:].rearrange("p (y x) -> p y x", x=SIDE)
+                for j in range(KSIZE):
+                    dx = j - PAD
+                    lo = max(0, -dx)
+                    hi = SIDE - max(0, dx)
+                    engines[ct](
+                        out=shifted[:, j, ct, PAD : PAD + SIDE, lo:hi],
+                        in_=image[:, :, lo + dx : hi + dx],
+                    )
+
+        project_channels_first("k", k_shift, (nc.scalar.copy, nc.vector.tensor_copy))
+
+        q_t = keep.tile([P, PIX_TILES, HEAD_DIM, HEADS], F32)
+        for t in range(PIX_TILES):
+            acc = sums.tile([P, D], F32, tag="sums")
+            cols = slice(t * P, (t + 1) * P)
+            for g in range(PASSES):
+                nc.tensor.matmul_mx(
+                    out=acc[:],
+                    lhsT=x_codes[:, g, cols].bitcast(FP8X4),
+                    lhsT_scale=x_scales[:, g, cols],
+                    rhs=w_codes["q"][:, g, :].bitcast(FP8X4),
+                    rhs_scale=w_scales["q"][:, g, :],
+                    start=(g == 0),
+                    stop=(g == PASSES - 1),
+                )
+            nc.scalar.copy(out=q_t[:, t], in_=acc[:].rearrange("p (h c) -> p c h", h=HEADS))
+
+        project_channels_first("v", v_shift, (nc.scalar.copy, nc.scalar.copy))
+
+        def window(shifted, t, o, ct):
+            i, j = divmod(o, KSIZE)
+            return shifted[:, j, ct, t * ROWS + i : t * ROWS + i + ROWS, :].rearrange("p y x -> p (y x)")
+
+        def load_windows(shifted, t, o_first, o_count):
+            bank = stream.tile([P, 2, D], F32, tag="stream")
+            for oo in range(o_count):
+                for ct in range(CH_TILES):
+                    nc.tensor.transpose(
+                        bank[:, oo, ct * P : (ct + 1) * P], window(shifted, t, o_first + oo, ct), ident[:]
+                    )
+            return bank
+
+        scores = []
+        for t in range(PIX_TILES):
+            score_t = sums.tile([P, 2 * P], F32, tag="sums", name="score_t")
+            for grp, (o_lo, o_hi) in enumerate(((0, FULL_OFFSETS), (FULL_OFFSETS, WIN))):
+                qk = keep.tile([P, HEAD_DIM, P], F32, name="qk_%d_%d" % (t, grp))
+                used = (o_hi - o_lo) * HEADS
+                if used < P:
+                    nc.gpsimd.memset(qk[:, :, used:P], 0.0)
+                for o in range(o_lo, o_hi, 2):
+                    n = min(2, o_hi - o)
+                    kt = load_windows(k_shift, t, o, n)
+                    col = (o - o_lo) * HEADS
+                    nc.vector.tensor_tensor(
+                        out=qk[:, :, col : col + n * HEADS].rearrange("p c (o h) -> p c o h", o=n),
+                        in0=kt[:, 0:n, :].rearrange("p o (h c) -> p c o h", h=HEADS),
+                        in1=q_t[:, t].unsqueeze(2).to_broadcast([P, HEAD_DIM, n, HEADS]),
+                        op=ALU.mult,
+                    )
+                for c in range(HEAD_DIM):
+                    nc.tensor.matmul(
+                        out=score_t[:, grp * P : (grp + 1) * P],
+                        lhsT=qk[:, c, :],
+                        rhs=ident[:],
+                        is_transpose=True,
+                        start=(c == 0),
+                        stop=(c == HEAD_DIM - 1),
+                    )
+            score_t_sb = small.tile([P, 2 * P], F32)
+            nc.scalar.copy(out=score_t_sb[:], in_=score_t[:])
+            score = sums.tile([P, 2 * P], F32, tag="sums", name="score")
+            for grp in range(2):
+                cols = slice(grp * P, (grp + 1) * P)
+                nc.tensor.transpose(score[:, cols], score_t_sb[:, cols], ident[:])
+            scores.append(score)
+
+        out_view = out.rearrange("n (ct c) h w -> c (n ct) (h w)", ct=CH_TILES, c=P)
+        for t in range(PIX_TILES):
+            valid = scores[t][:, 0 : WIN * HEADS]
+            top = small.tile([P, HEADS], F32)
+            nc.vector.tensor_reduce(
+                out=top[:], in_=valid.rearrange("p (o h) -> p h o", h=HEADS), axis=AXIS_X, op=ALU.max
+            )
+            centred = small.tile([P, WIN, HEADS], F32)
+            nc.vector.tensor_tensor(
+                out=centred[:],
+                in0=valid.rearrange("p (o h) -> p o h", h=HEADS),
+                in1=top[:].unsqueeze(1).to_broadcast([P, WIN, HEADS]),
+                op=ALU.subtract,
+            )
+            e = small.tile([P, WIN, HEADS], F32)
+            nc.scalar.activation(out=e[:], in_=centred[:], func=ACT.Exp)
+            total = small.tile([P, HEADS], F32)
+            nc.vector.tensor_reduce(
+                out=total[:], in_=e[:].rearrange("p o h -> p h o"), axis=AXIS_X, op=ALU.add
+            )
+            inv = small.tile([P, HEADS], F32)
+            nc.vector.reciprocal(out=inv[:], in_=total[:])
+            att = small.tile([P, WIN, HEADS], F32)
+            nc.vector.tensor_tensor(
+                out=att[:], in0=e[:], in1=inv[:].unsqueeze(1).to_broadcast([P, WIN, HEADS]), op=ALU.mult
+            )
+
+            result = [sums.tile([P, P], F32, tag="sums", name="result_%d" % ct) for ct in range(CH_TILES)]
+            for o in range(0, WIN, 2):
+                n = min(2, WIN - o)
+                vt = load_windows(v_shift, t, o, n)
+                av = work.tile([P, 2, D], F32)
+                nc.vector.tensor_tensor(
+                    out=av[:, 0:n, :].rearrange("p o (h c) -> p o h c", h=HEADS),
+                    in0=vt[:, 0:n, :].rearrange("p o (h c) -> p o h c", h=HEADS),
+                    in1=att[:, o : o + n, :].unsqueeze(3).to_broadcast([P, n, HEADS, HEAD_DIM]),
+                    op=ALU.mult,
+                )
+                for oo in range(n):
+                    for ct in range(CH_TILES):
+                        nc.tensor.matmul(
+                            out=result[ct][:],
+                            lhsT=av[:, oo, ct * P : (ct + 1) * P],
+                            rhs=ident[:],
+                            is_transpose=True,
+                            start=(o + oo == 0),
+                            stop=(o + oo == WIN - 1),
+                        )
+            out_sb = small.tile([P, CH_TILES, P], F32)
+            for ct in range(CH_TILES):
+                nc.scalar.copy(out=out_sb[:, ct, :], in_=result[ct][:])
+            nc.sync.dma_start(out=out_view[:, :, t * P : (t + 1) * P], in_=out_sb[:])

@@ -27,7 +27,8 @@ WIN = KSIZE * KSIZE
 PIX_TILES = PIX // P
 ROWS = P // SIDE
 CH_TILES = D // P
-FULL_OFFSETS = P // HEADS
+HALF_HEAD = HEAD_DIM // CH_TILES
+GPSIMD_OFFSETS = 16
 
 FLOPS = 2 * 3 * D * C_IN * PIX + 2 * 2 * D * WIN * PIX
 
@@ -37,7 +38,7 @@ def tile_relation_s_kernel(tc, x, w_qkv, out):
     with ExitStack() as ctx:
         keep = ctx.enter_context(tc.tile_pool(name="keep", bufs=1))
         small = ctx.enter_context(tc.tile_pool(name="small", bufs=2))
-        work = ctx.enter_context(tc.tile_pool(name="work", bufs=4))
+        work = ctx.enter_context(tc.tile_pool(name="work", bufs=8))
         stream = ctx.enter_context(tc.psum_pool(name="stream", bufs=4))
         sums = ctx.enter_context(tc.psum_pool(name="sums", bufs=4))
 
@@ -55,9 +56,14 @@ def tile_relation_s_kernel(tc, x, w_qkv, out):
 
         ident = keep.tile([P, P], F32)
         make_identity(nc, ident[:])
-        k_shift = keep.tile([P, KSIZE, CH_TILES, SIDE + 2 * PAD, SIDE], F32)
+        split_heads = keep.tile([P, P], F32)
+        nc.vector.tensor_copy(
+            out=split_heads[:].rearrange("p (b h c) -> p b h c", b=CH_TILES, c=HALF_HEAD),
+            in_=ident[:].rearrange("p (h b c) -> p b h c", b=CH_TILES, c=HALF_HEAD),
+        )
+        k_pad = keep.tile([P, CH_TILES, SIDE + 2 * PAD, SIDE + 2 * PAD], F32)
+        nc.vector.memset(k_pad[:], 0.0)
         v_shift = keep.tile([P, KSIZE, CH_TILES, SIDE + 2 * PAD, SIDE], F32)
-        nc.vector.memset(k_shift[:], 0.0)
         nc.vector.memset(v_shift[:], 0.0)
         warm = keep.tile([P, 1], F32)
         nc.vector.memset(warm[:], 0.0)
@@ -74,169 +80,162 @@ def tile_relation_s_kernel(tc, x, w_qkv, out):
             in_=x_grouped[:].rearrange("p g w t -> p (g w t)"),
         )
 
-        w_codes = {}
-        w_scales = {}
+        projected = {}
         for part in ("k", "q", "v"):
-            w_grouped = keep.tile([P, PASSES, D, PACK], BF16, align_bytes=64, name="w_grouped_" + part)
-            for ct in range(CH_TILES):
-                wt = stream.tile([P, PASSES * 2, P], F32, tag="stream")
-                words = w_sb[part][:, ct, :].bitcast(F32)
-                for gu in range(PASSES * 2):
-                    nc.tensor.transpose(wt[:, gu, :], words[:, gu * P : (gu + 1) * P], ident[:])
-                copy_out = nc.vector.tensor_copy if ct == 0 else nc.scalar.copy
-                copy_out(
-                    out=w_grouped[:].bitcast(F32)[:, :, ct * P : (ct + 1) * P, :],
-                    in_=wt[:].rearrange("p (g u) o -> p g o u", g=PASSES, u=2),
-                )
-            w_codes[part] = keep.tile([P, PASSES, D], U32, align_bytes=64, name="w_codes_" + part)
-            w_scales[part] = keep.tile([P, PASSES, D], U8, align_bytes=64, name="w_scales_" + part)
+            w_grouped = keep.tile([P, CH_TILES, PASSES, P, PACK], BF16, align_bytes=64, name="w_grouped_" + part)
+            w_words = w_grouped[:].bitcast(F32)
+            for a in range(CH_TILES):
+                wt = stream.tile([P, PASSES, 2, P], F32, tag="stream")
+                words = w_sb[part][:, a, :].bitcast(F32)
+                order = ident if part == "v" else split_heads
+                for g in range(PASSES):
+                    for u in range(2):
+                        first = (2 * g + u) * P
+                        nc.tensor.transpose(wt[:, g, u, :], words[:, first : first + P], order[:])
+                copy_out = nc.vector.tensor_copy if a == 0 else nc.scalar.copy
+                for g in range(PASSES):
+                    if part == "v":
+                        copy_out(out=w_words[:, a, g, :, :], in_=wt[:, g].rearrange("p u o -> p o u"))
+                    else:
+                        n = P // CH_TILES
+                        copy_out(
+                            out=w_words[:, :, g, a * n : (a + 1) * n, :],
+                            in_=wt[:, g].rearrange("p u (b o) -> p b o u", b=CH_TILES),
+                        )
+            w_codes = keep.tile([P, CH_TILES, PASSES, P], U32, align_bytes=64, name="w_codes_" + part)
+            w_scales = keep.tile([P, CH_TILES, PASSES, P], U8, align_bytes=64, name="w_scales_" + part)
             nc.vector.quantize_mx(
-                out=w_codes[part][:].rearrange("p g o -> p (g o)").bitcast(FP8X4),
-                scales=w_scales[part][:].rearrange("p g o -> p (g o)"),
-                in_=w_grouped[:].rearrange("p g o t -> p (g o t)"),
+                out=w_codes[:].rearrange("p b g o -> p (b g o)").bitcast(FP8X4),
+                scales=w_scales[:].rearrange("p b g o -> p (b g o)"),
+                in_=w_grouped[:].rearrange("p b g o t -> p (b g o t)"),
             )
-
-        def project_channels_first(part, shifted, engines):
-            for ct in range(CH_TILES):
-                acc = sums.tile([P, PIX], F32, tag="sums")
-                cols = slice(ct * P, (ct + 1) * P)
+            projected[part] = sums.tile([P, CH_TILES, PIX], F32, tag="sums", name="projected_" + part)
+            for b in range(CH_TILES):
                 for g in range(PASSES):
                     nc.tensor.matmul_mx(
-                        out=acc[:],
-                        lhsT=w_codes[part][:, g, cols].bitcast(FP8X4),
-                        lhsT_scale=w_scales[part][:, g, cols],
+                        out=projected[part][:, b, :],
+                        lhsT=w_codes[:, b, g, :].bitcast(FP8X4),
+                        lhsT_scale=w_scales[:, b, g, :],
                         rhs=x_codes[:, g, :].bitcast(FP8X4),
                         rhs_scale=x_scales[:, g, :],
                         start=(g == 0),
                         stop=(g == PASSES - 1),
                     )
-                image = acc[:].rearrange("p (y x) -> p y x", x=SIDE)
-                for j in range(KSIZE):
-                    dx = j - PAD
-                    lo = max(0, -dx)
-                    hi = SIDE - max(0, dx)
-                    engines[ct](
-                        out=shifted[:, j, ct, PAD : PAD + SIDE, lo:hi],
-                        in_=image[:, :, lo + dx : hi + dx],
-                    )
 
-        project_channels_first("k", k_shift, (nc.scalar.copy, nc.vector.tensor_copy))
+        nc.scalar.copy(
+            out=k_pad[:, :, PAD : PAD + SIDE, PAD : PAD + SIDE],
+            in_=projected["k"][:].rearrange("p b (y x) -> p b y x", x=SIDE),
+        )
+        q_psum = projected["q"][:].rearrange("p b (y x) -> p b y x", x=SIDE)
+        q_sb = keep.tile([P, CH_TILES, SIDE, SIDE], F32)
+        nc.vector.tensor_copy(out=q_sb[:], in_=q_psum)
+        v_image = projected["v"][:].rearrange("p b (y x) -> p b y x", x=SIDE)
+        for j in range(KSIZE):
+            dx = j - PAD
+            lo = max(0, -dx)
+            hi = SIDE - max(0, dx)
+            nc.scalar.copy(out=v_shift[:, j, :, PAD : PAD + SIDE, lo:hi], in_=v_image[:, :, :, lo + dx : hi + dx])
 
-        q_t = keep.tile([P, PIX_TILES, HEAD_DIM, HEADS], F32)
-        for t in range(PIX_TILES):
-            acc = sums.tile([P, D], F32, tag="sums")
-            cols = slice(t * P, (t + 1) * P)
-            for g in range(PASSES):
-                nc.tensor.matmul_mx(
-                    out=acc[:],
-                    lhsT=x_codes[:, g, cols].bitcast(FP8X4),
-                    lhsT_scale=x_scales[:, g, cols],
-                    rhs=w_codes["q"][:, g, :].bitcast(FP8X4),
-                    rhs_scale=w_scales["q"][:, g, :],
-                    start=(g == 0),
-                    stop=(g == PASSES - 1),
-                )
-            nc.scalar.copy(out=q_t[:, t], in_=acc[:].rearrange("p (h c) -> p c h", h=HEADS))
+        rows_of_softmax = PIX_TILES * HEADS
+        scores = keep.tile([P, WIN, rows_of_softmax], F32)
+        for o_first in range(0, WIN, 2):
+            n = min(2, WIN - o_first)
+            halves = stream.tile([P, 2, PIX_TILES, P], F32, tag="stream")
+            for oo in range(n):
+                i, j = divmod(o_first + oo, KSIZE)
+                k_window = k_pad[:, :, i : i + SIDE, j : j + SIDE]
+                qk = work.tile([P, CH_TILES, PIX], F32)
+                qk_image = qk[:].rearrange("p b (y x) -> p b y x", x=SIDE)
+                if oo == 0:
+                    nc.vector.tensor_tensor(out=qk_image, in0=q_psum, in1=k_window, op=ALU.mult)
+                else:
+                    nc.gpsimd.tensor_tensor(out=qk_image, in0=q_sb[:], in1=k_window, op=ALU.mult)
+                for t in range(PIX_TILES):
+                    for b in range(CH_TILES):
+                        nc.tensor.matmul(
+                            out=halves[:, oo, t, :],
+                            lhsT=qk[:, b, t * P : (t + 1) * P],
+                            rhs=ident[:],
+                            is_transpose=True,
+                            start=(b == 0),
+                            stop=(b == CH_TILES - 1),
+                        )
+            nc.vector.tensor_reduce(
+                out=scores[:, o_first : o_first + n, :].rearrange("p o r -> p (o r)"),
+                in_=halves[:, 0:n].rearrange("p o t (h c) -> p (o t h) c", c=HALF_HEAD),
+                axis=AXIS_X,
+                op=ALU.add,
+            )
 
-        project_channels_first("v", v_shift, (nc.scalar.copy, nc.scalar.copy))
-
-        def window(shifted, t, o, ct):
-            i, j = divmod(o, KSIZE)
-            return shifted[:, j, ct, t * ROWS + i : t * ROWS + i + ROWS, :].rearrange("p y x -> p (y x)")
-
-        def load_windows(shifted, t, o_first, o_count):
-            bank = stream.tile([P, 2, D], F32, tag="stream")
-            for oo in range(o_count):
-                for ct in range(CH_TILES):
-                    nc.tensor.transpose(
-                        bank[:, oo, ct * P : (ct + 1) * P], window(shifted, t, o_first + oo, ct), ident[:]
-                    )
-            return bank
-
-        scores = []
-        for t in range(PIX_TILES):
-            score_t = sums.tile([P, 2 * P], F32, tag="sums", name="score_t")
-            for grp, (o_lo, o_hi) in enumerate(((0, FULL_OFFSETS), (FULL_OFFSETS, WIN))):
-                qk = keep.tile([P, HEAD_DIM, P], F32, name="qk_%d_%d" % (t, grp))
-                used = (o_hi - o_lo) * HEADS
-                if used < P:
-                    nc.gpsimd.memset(qk[:, :, used:P], 0.0)
-                for o in range(o_lo, o_hi, 2):
-                    n = min(2, o_hi - o)
-                    kt = load_windows(k_shift, t, o, n)
-                    col = (o - o_lo) * HEADS
-                    nc.vector.tensor_tensor(
-                        out=qk[:, :, col : col + n * HEADS].rearrange("p c (o h) -> p c o h", o=n),
-                        in0=kt[:, 0:n, :].rearrange("p o (h c) -> p c o h", h=HEADS),
-                        in1=q_t[:, t].unsqueeze(2).to_broadcast([P, HEAD_DIM, n, HEADS]),
-                        op=ALU.mult,
-                    )
-                for c in range(HEAD_DIM):
-                    nc.tensor.matmul(
-                        out=score_t[:, grp * P : (grp + 1) * P],
-                        lhsT=qk[:, c, :],
-                        rhs=ident[:],
-                        is_transpose=True,
-                        start=(c == 0),
-                        stop=(c == HEAD_DIM - 1),
-                    )
-            score_t_sb = small.tile([P, 2 * P], F32)
-            nc.scalar.copy(out=score_t_sb[:], in_=score_t[:])
-            score = sums.tile([P, 2 * P], F32, tag="sums", name="score")
-            for grp in range(2):
-                cols = slice(grp * P, (grp + 1) * P)
-                nc.tensor.transpose(score[:, cols], score_t_sb[:, cols], ident[:])
-            scores.append(score)
+        top = small.tile([P, rows_of_softmax], F32)
+        nc.vector.tensor_reduce(out=top[:], in_=scores[:].rearrange("p o r -> p r o"), axis=AXIS_X, op=ALU.max)
+        centred = keep.tile([P, WIN, rows_of_softmax], F32)
+        nc.vector.tensor_tensor(
+            out=centred[:],
+            in0=scores[:],
+            in1=top[:].unsqueeze(1).to_broadcast([P, WIN, rows_of_softmax]),
+            op=ALU.subtract,
+        )
+        e = keep.tile([P, WIN, rows_of_softmax], F32)
+        nc.scalar.activation(out=e[:], in_=centred[:], func=ACT.Exp)
+        total = small.tile([P, rows_of_softmax], F32)
+        nc.vector.tensor_reduce(out=total[:], in_=e[:].rearrange("p o r -> p r o"), axis=AXIS_X, op=ALU.add)
+        inv = small.tile([P, rows_of_softmax], F32)
+        nc.vector.reciprocal(out=inv[:], in_=total[:])
+        att = keep.tile([P, WIN, PIX_TILES, HEADS], F32)
+        nc.vector.tensor_tensor(
+            out=att[:].rearrange("p o t h -> p o (t h)"),
+            in0=e[:],
+            in1=inv[:].unsqueeze(1).to_broadcast([P, WIN, rows_of_softmax]),
+            op=ALU.mult,
+        )
 
         out_view = out.rearrange("n (ct c) h w -> c (n ct) (h w)", ct=CH_TILES, c=P)
         for t in range(PIX_TILES):
-            valid = scores[t][:, 0 : WIN * HEADS]
-            top = small.tile([P, HEADS], F32)
-            nc.vector.tensor_reduce(
-                out=top[:], in_=valid.rearrange("p (o h) -> p h o", h=HEADS), axis=AXIS_X, op=ALU.max
-            )
-            centred = small.tile([P, WIN, HEADS], F32)
-            nc.vector.tensor_tensor(
-                out=centred[:],
-                in0=valid.rearrange("p (o h) -> p o h", h=HEADS),
-                in1=top[:].unsqueeze(1).to_broadcast([P, WIN, HEADS]),
-                op=ALU.subtract,
-            )
-            e = small.tile([P, WIN, HEADS], F32)
-            nc.scalar.activation(out=e[:], in_=centred[:], func=ACT.Exp)
-            total = small.tile([P, HEADS], F32)
-            nc.vector.tensor_reduce(
-                out=total[:], in_=e[:].rearrange("p o h -> p h o"), axis=AXIS_X, op=ALU.add
-            )
-            inv = small.tile([P, HEADS], F32)
-            nc.vector.reciprocal(out=inv[:], in_=total[:])
-            att = small.tile([P, WIN, HEADS], F32)
-            nc.vector.tensor_tensor(
-                out=att[:], in0=e[:], in1=inv[:].unsqueeze(1).to_broadcast([P, WIN, HEADS]), op=ALU.mult
-            )
-
-            result = [sums.tile([P, P], F32, tag="sums", name="result_%d" % ct) for ct in range(CH_TILES)]
-            for o in range(0, WIN, 2):
-                n = min(2, WIN - o)
-                vt = load_windows(v_shift, t, o, n)
-                av = work.tile([P, 2, D], F32)
+            partial = small.tile([P, 3, D], F32)
+            late = small.tile([P, WIN - GPSIMD_OFFSETS, D], F32)
+            first_pair = None
+            for o_first in range(0, WIN, 2):
+                n = min(2, WIN - o_first)
+                vt = stream.tile([P, 2, D], F32, tag="stream")
+                for oo in range(n):
+                    i, j = divmod(o_first + oo, KSIZE)
+                    for ct in range(CH_TILES):
+                        rows = v_shift[:, j, ct, t * ROWS + i : t * ROWS + i + ROWS, :]
+                        nc.tensor.transpose(
+                            vt[:, oo, ct * P : (ct + 1) * P], rows.rearrange("p y x -> p (y x)"), ident[:]
+                        )
+                if o_first < GPSIMD_OFFSETS:
+                    av = work.tile([P, 2, D], F32)
+                    weighted = av[:]
+                else:
+                    weighted = late[:, o_first - GPSIMD_OFFSETS : o_first - GPSIMD_OFFSETS + n, :]
                 nc.vector.tensor_tensor(
-                    out=av[:, 0:n, :].rearrange("p o (h c) -> p o h c", h=HEADS),
+                    out=weighted.rearrange("p o (h c) -> p o h c", h=HEADS),
                     in0=vt[:, 0:n, :].rearrange("p o (h c) -> p o h c", h=HEADS),
-                    in1=att[:, o : o + n, :].unsqueeze(3).to_broadcast([P, n, HEADS, HEAD_DIM]),
+                    in1=att[:, o_first : o_first + n, t, :].unsqueeze(3).to_broadcast([P, n, HEADS, HEAD_DIM]),
                     op=ALU.mult,
                 )
-                for oo in range(n):
-                    for ct in range(CH_TILES):
-                        nc.tensor.matmul(
-                            out=result[ct][:],
-                            lhsT=av[:, oo, ct * P : (ct + 1) * P],
-                            rhs=ident[:],
-                            is_transpose=True,
-                            start=(o + oo == 0),
-                            stop=(o + oo == WIN - 1),
-                        )
-            out_sb = small.tile([P, CH_TILES, P], F32)
+                if o_first == 0:
+                    first_pair = av
+                elif o_first == 2:
+                    nc.gpsimd.tensor_tensor(out=partial[:, 0:2, :], in0=first_pair[:], in1=av[:], op=ALU.add)
+                elif o_first < GPSIMD_OFFSETS:
+                    nc.gpsimd.tensor_tensor(out=partial[:, 0:2, :], in0=partial[:, 0:2, :], in1=av[:], op=ALU.add)
+            nc.vector.tensor_reduce(
+                out=partial[:, 2, :], in_=late[:].rearrange("p o c -> p c o"), axis=AXIS_X, op=ALU.add
+            )
+            result = sums.tile([P, CH_TILES, P], F32, tag="sums")
             for ct in range(CH_TILES):
-                nc.scalar.copy(out=out_sb[:, ct, :], in_=result[ct][:])
+                for s in range(3):
+                    nc.tensor.matmul(
+                        out=result[:, ct, :],
+                        lhsT=partial[:, s, ct * P : (ct + 1) * P],
+                        rhs=ident[:],
+                        is_transpose=True,
+                        start=(s == 0),
+                        stop=(s == 2),
+                    )
+            out_sb = small.tile([P, CH_TILES, P], F32)
+            nc.scalar.copy(out=out_sb[:], in_=result[:])
             nc.sync.dma_start(out=out_view[:, :, t * P : (t + 1) * P], in_=out_sb[:])

@@ -51,8 +51,9 @@ def tile_relation_s_kernel(tc, x, w_qkv, out):
         w_sb = {}
         for part in ("k", "q", "v"):
             w_sb[part] = keep.tile([P, CH_TILES, C_IN], BF16, name="w_sb_" + part)
-            rows = w_qkv[first_row[part] : first_row[part] + D, :]
-            nc.sync.dma_start(out=w_sb[part][:], in_=rows.rearrange("(a p) k -> p a k", p=P))
+            for a in range(CH_TILES):
+                row = first_row[part] + a * P
+                nc.sync.dma_start(out=w_sb[part][:, a, :], in_=w_qkv[row : row + P, :])
 
         ident = keep.tile([P, P], F32)
         make_identity(nc, ident[:])
@@ -62,9 +63,9 @@ def tile_relation_s_kernel(tc, x, w_qkv, out):
             in_=ident[:].rearrange("p (h b c) -> p b h c", b=CH_TILES, c=HALF_HEAD),
         )
         k_pad = keep.tile([P, CH_TILES, SIDE + 2 * PAD, SIDE + 2 * PAD], F32)
-        nc.vector.memset(k_pad[:], 0.0)
+        nc.gpsimd.memset(k_pad[:], 0.0)
         v_shift = keep.tile([P, KSIZE, CH_TILES, SIDE + 2 * PAD, SIDE], F32)
-        nc.vector.memset(v_shift[:], 0.0)
+        nc.gpsimd.memset(v_shift[:], 0.0)
         warm = keep.tile([P, 1], F32)
         nc.vector.memset(warm[:], 0.0)
         warm_out = keep.tile([P, 1], F32)
@@ -80,8 +81,7 @@ def tile_relation_s_kernel(tc, x, w_qkv, out):
             in_=x_grouped[:].rearrange("p g w t -> p (g w t)"),
         )
 
-        projected = {}
-        for part in ("k", "q", "v"):
+        def project(part):
             w_grouped = keep.tile([P, CH_TILES, PASSES, P, PACK], BF16, align_bytes=64, name="w_grouped_" + part)
             w_words = w_grouped[:].bitcast(F32)
             for a in range(CH_TILES):
@@ -109,11 +109,11 @@ def tile_relation_s_kernel(tc, x, w_qkv, out):
                 scales=w_scales[:].rearrange("p b g o -> p (b g o)"),
                 in_=w_grouped[:].rearrange("p b g o t -> p (b g o t)"),
             )
-            projected[part] = sums.tile([P, CH_TILES, PIX], F32, tag="sums", name="projected_" + part)
+            projected = sums.tile([P, CH_TILES, PIX], F32, tag="sums", name="projected_" + part)
             for b in range(CH_TILES):
                 for g in range(PASSES):
                     nc.tensor.matmul_mx(
-                        out=projected[part][:, b, :],
+                        out=projected[:, b, :],
                         lhsT=w_codes[:, b, g, :].bitcast(FP8X4),
                         lhsT_scale=w_scales[:, b, g, :],
                         rhs=x_codes[:, g, :].bitcast(FP8X4),
@@ -121,20 +121,12 @@ def tile_relation_s_kernel(tc, x, w_qkv, out):
                         start=(g == 0),
                         stop=(g == PASSES - 1),
                     )
+            return projected[:].rearrange("p b (y x) -> p b y x", x=SIDE)
 
-        nc.scalar.copy(
-            out=k_pad[:, :, PAD : PAD + SIDE, PAD : PAD + SIDE],
-            in_=projected["k"][:].rearrange("p b (y x) -> p b y x", x=SIDE),
-        )
-        q_psum = projected["q"][:].rearrange("p b (y x) -> p b y x", x=SIDE)
+        nc.scalar.copy(out=k_pad[:, :, PAD : PAD + SIDE, PAD : PAD + SIDE], in_=project("k"))
+        q_psum = project("q")
         q_sb = keep.tile([P, CH_TILES, SIDE, SIDE], F32)
         nc.vector.tensor_copy(out=q_sb[:], in_=q_psum)
-        v_image = projected["v"][:].rearrange("p b (y x) -> p b y x", x=SIDE)
-        for j in range(KSIZE):
-            dx = j - PAD
-            lo = max(0, -dx)
-            hi = SIDE - max(0, dx)
-            nc.scalar.copy(out=v_shift[:, j, :, PAD : PAD + SIDE, lo:hi], in_=v_image[:, :, :, lo + dx : hi + dx])
 
         rows_of_softmax = PIX_TILES * HEADS
         scores = keep.tile([P, WIN, rows_of_softmax], F32)
@@ -167,6 +159,13 @@ def tile_relation_s_kernel(tc, x, w_qkv, out):
                 op=ALU.add,
             )
 
+        v_image = project("v")
+        for j in range(KSIZE):
+            dx = j - PAD
+            lo = max(0, -dx)
+            hi = SIDE - max(0, dx)
+            nc.scalar.copy(out=v_shift[:, j, :, PAD : PAD + SIDE, lo:hi], in_=v_image[:, :, :, lo + dx : hi + dx])
+
         top = small.tile([P, rows_of_softmax], F32)
         nc.vector.tensor_reduce(out=top[:], in_=scores[:].rearrange("p o r -> p r o"), axis=AXIS_X, op=ALU.max)
         centred = keep.tile([P, WIN, rows_of_softmax], F32)
@@ -192,8 +191,8 @@ def tile_relation_s_kernel(tc, x, w_qkv, out):
 
         out_view = out.rearrange("n (ct c) h w -> c (n ct) (h w)", ct=CH_TILES, c=P)
         for t in range(PIX_TILES):
-            partial = small.tile([P, 3, D], F32)
-            late = small.tile([P, WIN - GPSIMD_OFFSETS, D], F32)
+            result = [sums.tile([P, P], F32, tag="sums", name="result_%d" % ct) for ct in range(CH_TILES)]
+            running = small.tile([P, 2, D], F32)
             first_pair = None
             for o_first in range(0, WIN, 2):
                 n = min(2, WIN - o_first)
@@ -205,13 +204,9 @@ def tile_relation_s_kernel(tc, x, w_qkv, out):
                         nc.tensor.transpose(
                             vt[:, oo, ct * P : (ct + 1) * P], rows.rearrange("p y x -> p (y x)"), ident[:]
                         )
-                if o_first < GPSIMD_OFFSETS:
-                    av = work.tile([P, 2, D], F32)
-                    weighted = av[:]
-                else:
-                    weighted = late[:, o_first - GPSIMD_OFFSETS : o_first - GPSIMD_OFFSETS + n, :]
+                av = work.tile([P, 2, D], F32)
                 nc.vector.tensor_tensor(
-                    out=weighted.rearrange("p o (h c) -> p o h c", h=HEADS),
+                    out=av[:, 0:n, :].rearrange("p o (h c) -> p o h c", h=HEADS),
                     in0=vt[:, 0:n, :].rearrange("p o (h c) -> p o h c", h=HEADS),
                     in1=att[:, o_first : o_first + n, t, :].unsqueeze(3).to_broadcast([P, n, HEADS, HEAD_DIM]),
                     op=ALU.mult,
@@ -219,23 +214,30 @@ def tile_relation_s_kernel(tc, x, w_qkv, out):
                 if o_first == 0:
                     first_pair = av
                 elif o_first == 2:
-                    nc.gpsimd.tensor_tensor(out=partial[:, 0:2, :], in0=first_pair[:], in1=av[:], op=ALU.add)
+                    nc.gpsimd.tensor_tensor(out=running[:], in0=first_pair[:], in1=av[:], op=ALU.add)
                 elif o_first < GPSIMD_OFFSETS:
-                    nc.gpsimd.tensor_tensor(out=partial[:, 0:2, :], in0=partial[:, 0:2, :], in1=av[:], op=ALU.add)
-            nc.vector.tensor_reduce(
-                out=partial[:, 2, :], in_=late[:].rearrange("p o c -> p c o"), axis=AXIS_X, op=ALU.add
-            )
-            result = sums.tile([P, CH_TILES, P], F32, tag="sums")
+                    nc.gpsimd.tensor_tensor(out=running[:], in0=running[:], in1=av[:], op=ALU.add)
+                else:
+                    for oo in range(n):
+                        for ct in range(CH_TILES):
+                            nc.tensor.matmul(
+                                out=result[ct][:],
+                                lhsT=av[:, oo, ct * P : (ct + 1) * P],
+                                rhs=ident[:],
+                                is_transpose=True,
+                                start=(o_first + oo == GPSIMD_OFFSETS),
+                                stop=False,
+                            )
+            out_sb = small.tile([P, CH_TILES, P], F32)
             for ct in range(CH_TILES):
-                for s in range(3):
+                for s in range(2):
                     nc.tensor.matmul(
-                        out=result[:, ct, :],
-                        lhsT=partial[:, s, ct * P : (ct + 1) * P],
+                        out=result[ct][:],
+                        lhsT=running[:, s, ct * P : (ct + 1) * P],
                         rhs=ident[:],
                         is_transpose=True,
-                        start=(s == 0),
-                        stop=(s == 2),
+                        start=False,
+                        stop=(s == 1),
                     )
-            out_sb = small.tile([P, CH_TILES, P], F32)
-            nc.scalar.copy(out=out_sb[:], in_=result[:])
+                nc.scalar.copy(out=out_sb[:, ct, :], in_=result[ct][:])
             nc.sync.dma_start(out=out_view[:, :, t * P : (t + 1) * P], in_=out_sb[:])

@@ -11,6 +11,7 @@ FP8X4 = mybir.dt.float8_e4m3fn_x4
 ALU = mybir.AluOpType
 ACT = mybir.ActivationFunctionType
 AXIS_X = mybir.AxisListType.X
+AXIS_XY = mybir.AxisListType.XY
 
 P = 128
 PACK = 4
@@ -28,7 +29,6 @@ PIX_TILES = PIX // P
 ROWS = P // SIDE
 CH_TILES = D // P
 HALF_HEAD = HEAD_DIM // CH_TILES
-GPSIMD_OFFSETS = 16
 
 FLOPS = 2 * 3 * D * C_IN * PIX + 2 * 2 * D * WIN * PIX
 
@@ -38,7 +38,7 @@ def tile_relation_s_kernel(tc, x, w_qkv, out):
     with ExitStack() as ctx:
         keep = ctx.enter_context(tc.tile_pool(name="keep", bufs=1))
         small = ctx.enter_context(tc.tile_pool(name="small", bufs=2))
-        work = ctx.enter_context(tc.tile_pool(name="work", bufs=8))
+        work = ctx.enter_context(tc.tile_pool(name="work", bufs=4))
         stream = ctx.enter_context(tc.psum_pool(name="stream", bufs=4))
         sums = ctx.enter_context(tc.psum_pool(name="sums", bufs=4))
 
@@ -64,8 +64,16 @@ def tile_relation_s_kernel(tc, x, w_qkv, out):
         )
         k_pad = keep.tile([P, CH_TILES, SIDE + 2 * PAD, SIDE + 2 * PAD], F32)
         nc.gpsimd.memset(k_pad[:], 0.0)
-        v_shift = keep.tile([P, KSIZE, CH_TILES, SIDE + 2 * PAD, SIDE], F32)
-        nc.gpsimd.memset(v_shift[:], 0.0)
+        inside = keep.tile([P, KSIZE], F32)
+        for j in range(KSIZE):
+            lo = max(0, PAD - j)
+            hi = SIDE - max(0, j - PAD)
+            nc.vector.tensor_reduce(
+                out=inside[:, j : j + 1],
+                in_=ident[:].rearrange("p (y x) -> p y x", x=SIDE)[:, :, lo:hi],
+                axis=AXIS_XY,
+                op=ALU.add,
+            )
         warm = keep.tile([P, 1], F32)
         nc.vector.memset(warm[:], 0.0)
         warm_out = keep.tile([P, 1], F32)
@@ -81,34 +89,45 @@ def tile_relation_s_kernel(tc, x, w_qkv, out):
             in_=x_grouped[:].rearrange("p g w t -> p (g w t)"),
         )
 
-        def project(part):
-            w_grouped = keep.tile([P, CH_TILES, PASSES, P, PACK], BF16, align_bytes=64, name="w_grouped_" + part)
+        def quantise_weight(part, split):
+            w_grouped = keep.tile([P, PASSES * D * PACK], BF16, align_bytes=64, name="w_grouped_" + part)
             w_words = w_grouped[:].bitcast(F32)
             for a in range(CH_TILES):
                 wt = stream.tile([P, PASSES, 2, P], F32, tag="stream")
                 words = w_sb[part][:, a, :].bitcast(F32)
-                order = ident if part == "v" else split_heads
+                order = split_heads if split else ident
                 for g in range(PASSES):
                     for u in range(2):
                         first = (2 * g + u) * P
                         nc.tensor.transpose(wt[:, g, u, :], words[:, first : first + P], order[:])
                 copy_out = nc.vector.tensor_copy if a == 0 else nc.scalar.copy
                 for g in range(PASSES):
-                    if part == "v":
-                        copy_out(out=w_words[:, a, g, :, :], in_=wt[:, g].rearrange("p u o -> p o u"))
-                    else:
+                    if split:
                         n = P // CH_TILES
                         copy_out(
-                            out=w_words[:, :, g, a * n : (a + 1) * n, :],
+                            out=w_words.rearrange("p (b g o u) -> p b g o u", b=CH_TILES, g=PASSES, u=2)[
+                                :, :, g, a * n : (a + 1) * n, :
+                            ],
                             in_=wt[:, g].rearrange("p u (b o) -> p b o u", b=CH_TILES),
                         )
-            w_codes = keep.tile([P, CH_TILES, PASSES, P], U32, align_bytes=64, name="w_codes_" + part)
-            w_scales = keep.tile([P, CH_TILES, PASSES, P], U8, align_bytes=64, name="w_scales_" + part)
-            nc.vector.quantize_mx(
-                out=w_codes[:].rearrange("p b g o -> p (b g o)").bitcast(FP8X4),
-                scales=w_scales[:].rearrange("p b g o -> p (b g o)"),
-                in_=w_grouped[:].rearrange("p b g o t -> p (b g o t)"),
-            )
+                    else:
+                        copy_out(
+                            out=w_words.rearrange("p (g o u) -> p g o u", g=PASSES, u=2)[:, g, a * P : (a + 1) * P, :],
+                            in_=wt[:, g].rearrange("p u o -> p o u"),
+                        )
+            w_codes = keep.tile([P, PASSES * D], U32, align_bytes=64, name="w_codes_" + part)
+            w_scales = keep.tile([P, PASSES * D], U8, align_bytes=64, name="w_scales_" + part)
+            nc.vector.quantize_mx(out=w_codes[:].bitcast(FP8X4), scales=w_scales[:], in_=w_grouped[:])
+            if split:
+                shape = "p (b g o) -> p b g o"
+                return (
+                    w_codes[:].rearrange(shape, b=CH_TILES, g=PASSES),
+                    w_scales[:].rearrange(shape, b=CH_TILES, g=PASSES),
+                )
+            return w_codes[:].rearrange("p (g o) -> p g o", g=PASSES), w_scales[:].rearrange("p (g o) -> p g o", g=PASSES)
+
+        def project_channels_first(part):
+            w_codes, w_scales = quantise_weight(part, True)
             projected = sums.tile([P, CH_TILES, PIX], F32, tag="sums", name="projected_" + part)
             for b in range(CH_TILES):
                 for g in range(PASSES):
@@ -123,10 +142,48 @@ def tile_relation_s_kernel(tc, x, w_qkv, out):
                     )
             return projected[:].rearrange("p b (y x) -> p b y x", x=SIDE)
 
-        nc.scalar.copy(out=k_pad[:, :, PAD : PAD + SIDE, PAD : PAD + SIDE], in_=project("k"))
-        q_psum = project("q")
+        nc.scalar.copy(out=k_pad[:, :, PAD : PAD + SIDE, PAD : PAD + SIDE], in_=project_channels_first("k"))
+        q_psum = project_channels_first("q")
         q_sb = keep.tile([P, CH_TILES, SIDE, SIDE], F32)
         nc.vector.tensor_copy(out=q_sb[:], in_=q_psum)
+
+        parked = out.rearrange("n c h w -> (n c) (h w)")
+        v_codes, v_scales = quantise_weight("v", False)
+        v_sb = keep.tile([P, PIX_TILES, D], F32)
+        for t in range(PIX_TILES):
+            v_psum = sums.tile([P, D], F32, tag="sums")
+            cols = slice(t * P, (t + 1) * P)
+            for g in range(PASSES):
+                nc.tensor.matmul_mx(
+                    out=v_psum[:],
+                    lhsT=x_codes[:, g, cols].bitcast(FP8X4),
+                    lhsT_scale=x_scales[:, g, cols],
+                    rhs=v_codes[:, g, :].bitcast(FP8X4),
+                    rhs_scale=v_scales[:, g, :],
+                    start=(g == 0),
+                    stop=(g == PASSES - 1),
+                )
+            nc.scalar.copy(out=v_sb[:, t, :], in_=v_psum[:])
+        nc.sync.dma_start(out=parked.rearrange("(t p) c -> p t c", p=P), in_=v_sb[:])
+
+        v_win = keep.tile([P, PIX_TILES, WIN, D], F32)
+        centre = WIN // 2
+        nc.gpsimd.memset(v_win[0 : P // 2, 0, 0:centre, :], 0.0)
+        nc.gpsimd.memset(v_win[P // 2 : P, PIX_TILES - 1, centre + 1 : WIN, :], 0.0)
+        for t in range(PIX_TILES):
+            for o in range(WIN):
+                i, j = divmod(o, KSIZE)
+                top_row = t * ROWS + i - PAD
+                first = top_row * SIDE + j - PAD
+                lo = max(0, -top_row) * SIDE
+                hi = min(ROWS, SIDE - top_row) * SIDE
+                pieces = [(lo, hi)]
+                if first + lo < 0:
+                    pieces = [(-first, lo + SIDE), (lo + SIDE, hi)]
+                if first + hi > PIX:
+                    pieces = [(lo, hi - SIDE), (hi - SIDE, PIX - first)]
+                for p_lo, p_hi in pieces:
+                    nc.sync.dma_start(out=v_win[p_lo:p_hi, t, o, :], in_=parked[first + p_lo : first + p_hi, :])
 
         rows_of_softmax = PIX_TILES * HEADS
         scores = keep.tile([P, WIN, rows_of_softmax], F32)
@@ -136,7 +193,7 @@ def tile_relation_s_kernel(tc, x, w_qkv, out):
             for oo in range(n):
                 i, j = divmod(o_first + oo, KSIZE)
                 k_window = k_pad[:, :, i : i + SIDE, j : j + SIDE]
-                qk = work.tile([P, CH_TILES, PIX], F32)
+                qk = work.tile([P, CH_TILES, PIX], F32, bufs=8)
                 qk_image = qk[:].rearrange("p b (y x) -> p b y x", x=SIDE)
                 if oo == 0:
                     nc.vector.tensor_tensor(out=qk_image, in0=q_psum, in1=k_window, op=ALU.mult)
@@ -159,13 +216,6 @@ def tile_relation_s_kernel(tc, x, w_qkv, out):
                 op=ALU.add,
             )
 
-        v_image = project("v")
-        for j in range(KSIZE):
-            dx = j - PAD
-            lo = max(0, -dx)
-            hi = SIDE - max(0, dx)
-            nc.scalar.copy(out=v_shift[:, j, :, PAD : PAD + SIDE, lo:hi], in_=v_image[:, :, :, lo + dx : hi + dx])
-
         top = small.tile([P, rows_of_softmax], F32)
         nc.vector.tensor_reduce(out=top[:], in_=scores[:].rearrange("p o r -> p r o"), axis=AXIS_X, op=ALU.max)
         centred = keep.tile([P, WIN, rows_of_softmax], F32)
@@ -181,63 +231,43 @@ def tile_relation_s_kernel(tc, x, w_qkv, out):
         nc.vector.tensor_reduce(out=total[:], in_=e[:].rearrange("p o r -> p r o"), axis=AXIS_X, op=ALU.add)
         inv = small.tile([P, rows_of_softmax], F32)
         nc.vector.reciprocal(out=inv[:], in_=total[:])
+        inv_inside = small.tile([P, KSIZE, rows_of_softmax], F32)
+        nc.vector.tensor_tensor(
+            out=inv_inside[:],
+            in0=inv[:].unsqueeze(1).to_broadcast([P, KSIZE, rows_of_softmax]),
+            in1=inside[:].unsqueeze(2).to_broadcast([P, KSIZE, rows_of_softmax]),
+            op=ALU.mult,
+        )
         att = keep.tile([P, WIN, PIX_TILES, HEADS], F32)
         nc.vector.tensor_tensor(
-            out=att[:].rearrange("p o t h -> p o (t h)"),
-            in0=e[:],
-            in1=inv[:].unsqueeze(1).to_broadcast([P, WIN, rows_of_softmax]),
+            out=att[:].rearrange("p (i j) t h -> p i (j t h)", j=KSIZE),
+            in0=e[:].rearrange("p (i j) r -> p i (j r)", j=KSIZE),
+            in1=inv_inside[:].rearrange("p j r -> p (j r)").unsqueeze(1).to_broadcast([P, KSIZE, KSIZE * rows_of_softmax]),
             op=ALU.mult,
         )
 
         out_view = out.rearrange("n (ct c) h w -> c (n ct) (h w)", ct=CH_TILES, c=P)
         for t in range(PIX_TILES):
             result = [sums.tile([P, P], F32, tag="sums", name="result_%d" % ct) for ct in range(CH_TILES)]
-            running = small.tile([P, 2, D], F32)
-            first_pair = None
-            for o_first in range(0, WIN, 2):
-                n = min(2, WIN - o_first)
-                vt = stream.tile([P, 2, D], F32, tag="stream")
-                for oo in range(n):
-                    i, j = divmod(o_first + oo, KSIZE)
-                    for ct in range(CH_TILES):
-                        rows = v_shift[:, j, ct, t * ROWS + i : t * ROWS + i + ROWS, :]
-                        nc.tensor.transpose(
-                            vt[:, oo, ct * P : (ct + 1) * P], rows.rearrange("p y x -> p (y x)"), ident[:]
-                        )
-                av = work.tile([P, 2, D], F32)
+            for o_first in range(0, WIN, KSIZE):
+                av = work.tile([P, KSIZE, D], F32)
                 nc.vector.tensor_tensor(
-                    out=av[:, 0:n, :].rearrange("p o (h c) -> p o h c", h=HEADS),
-                    in0=vt[:, 0:n, :].rearrange("p o (h c) -> p o h c", h=HEADS),
-                    in1=att[:, o_first : o_first + n, t, :].unsqueeze(3).to_broadcast([P, n, HEADS, HEAD_DIM]),
+                    out=av[:].rearrange("p o (h c) -> p o h c", h=HEADS),
+                    in0=v_win[:, t, o_first : o_first + KSIZE, :].rearrange("p o (h c) -> p o h c", h=HEADS),
+                    in1=att[:, o_first : o_first + KSIZE, t, :].unsqueeze(3).to_broadcast([P, KSIZE, HEADS, HEAD_DIM]),
                     op=ALU.mult,
                 )
-                if o_first == 0:
-                    first_pair = av
-                elif o_first == 2:
-                    nc.gpsimd.tensor_tensor(out=running[:], in0=first_pair[:], in1=av[:], op=ALU.add)
-                elif o_first < GPSIMD_OFFSETS:
-                    nc.gpsimd.tensor_tensor(out=running[:], in0=running[:], in1=av[:], op=ALU.add)
-                else:
-                    for oo in range(n):
-                        for ct in range(CH_TILES):
-                            nc.tensor.matmul(
-                                out=result[ct][:],
-                                lhsT=av[:, oo, ct * P : (ct + 1) * P],
-                                rhs=ident[:],
-                                is_transpose=True,
-                                start=(o_first + oo == GPSIMD_OFFSETS),
-                                stop=False,
-                            )
+                for oo in range(KSIZE):
+                    for ct in range(CH_TILES):
+                        nc.tensor.matmul(
+                            out=result[ct][:],
+                            lhsT=av[:, oo, ct * P : (ct + 1) * P],
+                            rhs=ident[:],
+                            is_transpose=True,
+                            start=(o_first + oo == 0),
+                            stop=(o_first + oo == WIN - 1),
+                        )
             out_sb = small.tile([P, CH_TILES, P], F32)
             for ct in range(CH_TILES):
-                for s in range(2):
-                    nc.tensor.matmul(
-                        out=result[ct][:],
-                        lhsT=running[:, s, ct * P : (ct + 1) * P],
-                        rhs=ident[:],
-                        is_transpose=True,
-                        start=False,
-                        stop=(s == 1),
-                    )
                 nc.scalar.copy(out=out_sb[:, ct, :], in_=result[ct][:])
             nc.sync.dma_start(out=out_view[:, :, t * P : (t + 1) * P], in_=out_sb[:])

@@ -49,7 +49,7 @@ def tile_relation_s_kernel(tc, x, w_qkv, out):
         )
         first_row = {"q": 0, "k": D, "v": 2 * D}
         w_sb = {}
-        for part in ("k", "q", "v"):
+        for part in ("v", "k", "q"):
             w_sb[part] = keep.tile([P, CH_TILES, C_IN], BF16, name="w_sb_" + part)
             for a in range(CH_TILES):
                 row = first_row[part] + a * P
@@ -63,7 +63,11 @@ def tile_relation_s_kernel(tc, x, w_qkv, out):
             in_=ident[:].rearrange("p (h b c) -> p b h c", b=CH_TILES, c=HALF_HEAD),
         )
         k_pad = keep.tile([P, CH_TILES, SIDE + 2 * PAD, SIDE + 2 * PAD], F32)
-        nc.gpsimd.memset(k_pad[:], 0.0)
+        nc.vector.memset(k_pad[:], 0.0)
+        v_win = keep.tile([P, PIX_TILES, WIN, D], F32)
+        centre = WIN // 2
+        nc.vector.memset(v_win[0 : P // 2, 0, 0:centre, :], 0.0)
+        nc.vector.memset(v_win[P // 2 : P, PIX_TILES - 1, centre + 1 : WIN, :], 0.0)
         inside = keep.tile([P, KSIZE], F32)
         for j in range(KSIZE):
             lo = max(0, PAD - j)
@@ -126,6 +130,40 @@ def tile_relation_s_kernel(tc, x, w_qkv, out):
                 )
             return w_codes[:].rearrange("p (g o) -> p g o", g=PASSES), w_scales[:].rearrange("p (g o) -> p g o", g=PASSES)
 
+        parked = out.rearrange("n c h w -> (n c) (h w)")
+        v_codes, v_scales = quantise_weight("v", False)
+        v_sb = keep.tile([P, PIX_TILES, D], F32)
+        for t in range(PIX_TILES):
+            v_psum = sums.tile([P, D], F32, tag="sums")
+            cols = slice(t * P, (t + 1) * P)
+            for g in range(PASSES):
+                nc.tensor.matmul_mx(
+                    out=v_psum[:],
+                    lhsT=x_codes[:, g, cols].bitcast(FP8X4),
+                    lhsT_scale=x_scales[:, g, cols],
+                    rhs=v_codes[:, g, :].bitcast(FP8X4),
+                    rhs_scale=v_scales[:, g, :],
+                    start=(g == 0),
+                    stop=(g == PASSES - 1),
+                )
+            nc.scalar.copy(out=v_sb[:, t, :], in_=v_psum[:])
+        nc.sync.dma_start(out=parked.rearrange("(t p) c -> p t c", p=P), in_=v_sb[:])
+
+        for t in range(PIX_TILES):
+            for o in range(WIN):
+                i, j = divmod(o, KSIZE)
+                top_row = t * ROWS + i - PAD
+                first = top_row * SIDE + j - PAD
+                lo = max(0, -top_row) * SIDE
+                hi = min(ROWS, SIDE - top_row) * SIDE
+                pieces = [(lo, hi)]
+                if first + lo < 0:
+                    pieces = [(-first, lo + SIDE), (lo + SIDE, hi)]
+                if first + hi > PIX:
+                    pieces = [(lo, hi - SIDE), (hi - SIDE, PIX - first)]
+                for p_lo, p_hi in pieces:
+                    nc.sync.dma_start(out=v_win[p_lo:p_hi, t, o, :], in_=parked[first + p_lo : first + p_hi, :])
+
         def project_channels_first(part):
             w_codes, w_scales = quantise_weight(part, True)
             projected = sums.tile([P, CH_TILES, PIX], F32, tag="sums", name="projected_" + part)
@@ -146,44 +184,6 @@ def tile_relation_s_kernel(tc, x, w_qkv, out):
         q_psum = project_channels_first("q")
         q_sb = keep.tile([P, CH_TILES, SIDE, SIDE], F32)
         nc.vector.tensor_copy(out=q_sb[:], in_=q_psum)
-
-        parked = out.rearrange("n c h w -> (n c) (h w)")
-        v_codes, v_scales = quantise_weight("v", False)
-        v_sb = keep.tile([P, PIX_TILES, D], F32)
-        for t in range(PIX_TILES):
-            v_psum = sums.tile([P, D], F32, tag="sums")
-            cols = slice(t * P, (t + 1) * P)
-            for g in range(PASSES):
-                nc.tensor.matmul_mx(
-                    out=v_psum[:],
-                    lhsT=x_codes[:, g, cols].bitcast(FP8X4),
-                    lhsT_scale=x_scales[:, g, cols],
-                    rhs=v_codes[:, g, :].bitcast(FP8X4),
-                    rhs_scale=v_scales[:, g, :],
-                    start=(g == 0),
-                    stop=(g == PASSES - 1),
-                )
-            nc.scalar.copy(out=v_sb[:, t, :], in_=v_psum[:])
-        nc.sync.dma_start(out=parked.rearrange("(t p) c -> p t c", p=P), in_=v_sb[:])
-
-        v_win = keep.tile([P, PIX_TILES, WIN, D], F32)
-        centre = WIN // 2
-        nc.gpsimd.memset(v_win[0 : P // 2, 0, 0:centre, :], 0.0)
-        nc.gpsimd.memset(v_win[P // 2 : P, PIX_TILES - 1, centre + 1 : WIN, :], 0.0)
-        for t in range(PIX_TILES):
-            for o in range(WIN):
-                i, j = divmod(o, KSIZE)
-                top_row = t * ROWS + i - PAD
-                first = top_row * SIDE + j - PAD
-                lo = max(0, -top_row) * SIDE
-                hi = min(ROWS, SIDE - top_row) * SIDE
-                pieces = [(lo, hi)]
-                if first + lo < 0:
-                    pieces = [(-first, lo + SIDE), (lo + SIDE, hi)]
-                if first + hi > PIX:
-                    pieces = [(lo, hi - SIDE), (hi - SIDE, PIX - first)]
-                for p_lo, p_hi in pieces:
-                    nc.sync.dma_start(out=v_win[p_lo:p_hi, t, o, :], in_=parked[first + p_lo : first + p_hi, :])
 
         rows_of_softmax = PIX_TILES * HEADS
         scores = keep.tile([P, WIN, rows_of_softmax], F32)

@@ -29,6 +29,7 @@ PIX_TILES = PIX // P
 ROWS = P // SIDE
 CH_TILES = D // P
 HALF_HEAD = HEAD_DIM // CH_TILES
+LAST_CUT = 3
 
 FLOPS = 2 * 3 * D * C_IN * PIX + 2 * 2 * D * WIN * PIX
 
@@ -66,8 +67,13 @@ def tile_relation_s_kernel(tc, x, w_qkv, out):
         nc.vector.memset(k_pad[:], 0.0)
         v_win = keep.tile([P, PIX_TILES, WIN, D], F32)
         centre = WIN // 2
-        nc.vector.memset(v_win[0 : P // 2, 0, 0:centre, :], 0.0)
-        nc.vector.memset(v_win[P // 2 : P, PIX_TILES - 1, centre + 1 : WIN, :], 0.0)
+        zero = keep.tile([P, 1], F32)
+        nc.vector.memset(zero[:], 0.0)
+        nc.scalar.copy(
+            out=v_win[0 : P // 2, 0, 0:centre, :],
+            in_=zero[0 : P // 2].unsqueeze(2).to_broadcast([P // 2, centre, D]),
+        )
+        nc.gpsimd.memset(v_win[P // 2 : P, PIX_TILES - 1, centre + 1 : WIN, :], 0.0)
         inside = keep.tile([P, KSIZE], F32)
         for j in range(KSIZE):
             lo = max(0, PAD - j)
@@ -78,10 +84,8 @@ def tile_relation_s_kernel(tc, x, w_qkv, out):
                 axis=AXIS_XY,
                 op=ALU.add,
             )
-        warm = keep.tile([P, 1], F32)
-        nc.vector.memset(warm[:], 0.0)
         warm_out = keep.tile([P, 1], F32)
-        nc.scalar.activation(out=warm_out[:], in_=warm[:], func=ACT.Exp)
+        nc.scalar.activation(out=warm_out[:], in_=zero[:], func=ACT.Exp)
 
         x_grouped = keep.tile([P, PASSES, PIX, PACK], BF16, align_bytes=64)
         nc.vector.tensor_copy(out=x_grouped[:], in_=x_sb[:].rearrange("p g t w -> p g w t"))
@@ -249,15 +253,18 @@ def tile_relation_s_kernel(tc, x, w_qkv, out):
         out_view = out.rearrange("n (ct c) h w -> c (n ct) (h w)", ct=CH_TILES, c=P)
         for t in range(PIX_TILES):
             result = [sums.tile([P, P], F32, tag="sums", name="result_%d" % ct) for ct in range(CH_TILES)]
-            for o_first in range(0, WIN, KSIZE):
+            chunks = [(o, KSIZE) for o in range(0, WIN, KSIZE)]
+            if t == PIX_TILES - 1:
+                chunks[-1:] = [(WIN - KSIZE, LAST_CUT), (WIN - KSIZE + LAST_CUT, KSIZE - LAST_CUT)]
+            for o_first, n in chunks:
                 av = work.tile([P, KSIZE, D], F32)
                 nc.vector.tensor_tensor(
-                    out=av[:].rearrange("p o (h c) -> p o h c", h=HEADS),
-                    in0=v_win[:, t, o_first : o_first + KSIZE, :].rearrange("p o (h c) -> p o h c", h=HEADS),
-                    in1=att[:, o_first : o_first + KSIZE, t, :].unsqueeze(3).to_broadcast([P, KSIZE, HEADS, HEAD_DIM]),
+                    out=av[:, 0:n, :].rearrange("p o (h c) -> p o h c", h=HEADS),
+                    in0=v_win[:, t, o_first : o_first + n, :].rearrange("p o (h c) -> p o h c", h=HEADS),
+                    in1=att[:, o_first : o_first + n, t, :].unsqueeze(3).to_broadcast([P, n, HEADS, HEAD_DIM]),
                     op=ALU.mult,
                 )
-                for oo in range(KSIZE):
+                for oo in range(n):
                     for ct in range(CH_TILES):
                         nc.tensor.matmul(
                             out=result[ct][:],

from contextlib import ExitStack

import concourse.mybir as mybir
from concourse.masks import make_identity

F32 = mybir.dt.float32
BF16 = mybir.dt.bfloat16
U32 = mybir.dt.uint32
U8 = mybir.dt.uint8
FP8X4 = mybir.dt.float8_e4m3fn_x4
ALU = mybir.AluOpType
ACT = mybir.ActivationFunctionType
AXIS_X = mybir.AxisListType.X
AXIS_XY = mybir.AxisListType.XY

P = 128
PACK = 4
C_IN = 1024
PASSES = C_IN // (P * PACK)
D = 256
HEADS = 8
HEAD_DIM = D // HEADS
SIDE = 16
PIX = SIDE * SIDE
KSIZE = 5
PAD = KSIZE // 2
WIN = KSIZE * KSIZE
PIX_TILES = PIX // P
ROWS = P // SIDE
CH_TILES = D // P
HALF_HEAD = HEAD_DIM // CH_TILES
LAST_CUT = 3

FLOPS = 2 * 3 * D * C_IN * PIX + 2 * 2 * D * WIN * PIX


def tile_relation_s_kernel(tc, x, w_qkv, out):
    nc = tc.nc
    with ExitStack() as ctx:
        keep = ctx.enter_context(tc.tile_pool(name="keep", bufs=1))
        small = ctx.enter_context(tc.tile_pool(name="small", bufs=2))
        work = ctx.enter_context(tc.tile_pool(name="work", bufs=4))
        stream = ctx.enter_context(tc.psum_pool(name="stream", bufs=4))
        sums = ctx.enter_context(tc.psum_pool(name="sums", bufs=4))

        x_sb = keep.tile([P, PASSES, PACK, PIX], BF16)
        nc.sync.dma_start(
            out=x_sb[:].rearrange("p g (u e) w -> p (g u) (e w)", u=2, e=2),
            in_=x.rearrange("n (a q e) h w -> q (n a) (e h w)", a=PASSES * 2, q=P, e=2),
        )
        first_row = {"q": 0, "k": D, "v": 2 * D}
        w_sb = {}
        for part in ("v", "k", "q"):
            w_sb[part] = keep.tile([P, CH_TILES, C_IN], BF16, name="w_sb_" + part)
            for a in range(CH_TILES):
                row = first_row[part] + a * P
                nc.sync.dma_start(out=w_sb[part][:, a, :], in_=w_qkv[row : row + P, :])

        ident = keep.tile([P, P], F32)
        make_identity(nc, ident[:])
        split_heads = keep.tile([P, P], F32)
        nc.vector.tensor_copy(
            out=split_heads[:].rearrange("p (b h c) -> p b h c", b=CH_TILES, c=HALF_HEAD),
            in_=ident[:].rearrange("p (h b c) -> p b h c", b=CH_TILES, c=HALF_HEAD),
        )
        k_pad = keep.tile([P, CH_TILES, SIDE + 2 * PAD, SIDE + 2 * PAD], F32)
        nc.vector.memset(k_pad[:], 0.0)
        v_win = keep.tile([P, PIX_TILES, WIN, D], F32)
        centre = WIN // 2
        zero = keep.tile([P, 1], F32)
        nc.vector.memset(zero[:], 0.0)
        nc.scalar.copy(
            out=v_win[0 : P // 2, 0, 0:centre, :],
            in_=zero[0 : P // 2].unsqueeze(2).to_broadcast([P // 2, centre, D]),
        )
        nc.gpsimd.memset(v_win[P // 2 : P, PIX_TILES - 1, centre + 1 : WIN, :], 0.0)
        inside = keep.tile([P, KSIZE], F32)
        for j in range(KSIZE):
            lo = max(0, PAD - j)
            hi = SIDE - max(0, j - PAD)
            nc.vector.tensor_reduce(
                out=inside[:, j : j + 1],
                in_=ident[:].rearrange("p (y x) -> p y x", x=SIDE)[:, :, lo:hi],
                axis=AXIS_XY,
                op=ALU.add,
            )
        warm_out = keep.tile([P, 1], F32)
        nc.scalar.activation(out=warm_out[:], in_=zero[:], func=ACT.Exp)

        x_grouped = keep.tile([P, PASSES, PIX, PACK], BF16, align_bytes=64)
        nc.vector.tensor_copy(out=x_grouped[:], in_=x_sb[:].rearrange("p g t w -> p g w t"))
        x_codes = keep.tile([P, PASSES, PIX], U32, align_bytes=64)
        x_scales = keep.tile([P, PASSES, PIX], U8, align_bytes=64)
        nc.vector.quantize_mx(
            out=x_codes[:].rearrange("p g w -> p (g w)").bitcast(FP8X4),
            scales=x_scales[:].rearrange("p g w -> p (g w)"),
            in_=x_grouped[:].rearrange("p g w t -> p (g w t)"),
        )

        def quantise_weight(part, split):
            w_grouped = keep.tile([P, PASSES * D * PACK], BF16, align_bytes=64, name="w_grouped_" + part)
            w_words = w_grouped[:].bitcast(F32)
            for a in range(CH_TILES):
                wt = stream.tile([P, PASSES, 2, P], F32, tag="stream")
                words = w_sb[part][:, a, :].bitcast(F32)
                order = split_heads if split else ident
                for g in range(PASSES):
                    for u in range(2):
                        first = (2 * g + u) * P
                        nc.tensor.transpose(wt[:, g, u, :], words[:, first : first + P], order[:])
                copy_out = nc.vector.tensor_copy if a == 0 else nc.scalar.copy
                for g in range(PASSES):
                    if split:
                        n = P // CH_TILES
                        copy_out(
                            out=w_words.rearrange("p (b g o u) -> p b g o u", b=CH_TILES, g=PASSES, u=2)[
                                :, :, g, a * n : (a + 1) * n, :
                            ],
                            in_=wt[:, g].rearrange("p u (b o) -> p b o u", b=CH_TILES),
                        )
                    else:
                        copy_out(
                            out=w_words.rearrange("p (g o u) -> p g o u", g=PASSES, u=2)[:, g, a * P : (a + 1) * P, :],
                            in_=wt[:, g].rearrange("p u o -> p o u"),
                        )
            w_codes = keep.tile([P, PASSES * D], U32, align_bytes=64, name="w_codes_" + part)
            w_scales = keep.tile([P, PASSES * D], U8, align_bytes=64, name="w_scales_" + part)
            nc.vector.quantize_mx(out=w_codes[:].bitcast(FP8X4), scales=w_scales[:], in_=w_grouped[:])
            if split:
                shape = "p (b g o) -> p b g o"
                return (
                    w_codes[:].rearrange(shape, b=CH_TILES, g=PASSES),
                    w_scales[:].rearrange(shape, b=CH_TILES, g=PASSES),
                )
            return w_codes[:].rearrange("p (g o) -> p g o", g=PASSES), w_scales[:].rearrange("p (g o) -> p g o", g=PASSES)

        parked = out.rearrange("n c h w -> (n c) (h w)")
        v_codes, v_scales = quantise_weight("v", False)
        v_sb = keep.tile([P, PIX_TILES, D], F32)
        for t in range(PIX_TILES):
            v_psum = sums.tile([P, D], F32, tag="sums")
            cols = slice(t * P, (t + 1) * P)
            for g in range(PASSES):
                nc.tensor.matmul_mx(
                    out=v_psum[:],
                    lhsT=x_codes[:, g, cols].bitcast(FP8X4),
                    lhsT_scale=x_scales[:, g, cols],
                    rhs=v_codes[:, g, :].bitcast(FP8X4),
                    rhs_scale=v_scales[:, g, :],
                    start=(g == 0),
                    stop=(g == PASSES - 1),
                )
            nc.scalar.copy(out=v_sb[:, t, :], in_=v_psum[:])
        nc.sync.dma_start(out=parked.rearrange("(t p) c -> p t c", p=P), in_=v_sb[:])

        for t in range(PIX_TILES):
            for o in range(WIN):
                i, j = divmod(o, KSIZE)
                top_row = t * ROWS + i - PAD
                first = top_row * SIDE + j - PAD
                lo = max(0, -top_row) * SIDE
                hi = min(ROWS, SIDE - top_row) * SIDE
                pieces = [(lo, hi)]
                if first + lo < 0:
                    pieces = [(-first, lo + SIDE), (lo + SIDE, hi)]
                if first + hi > PIX:
                    pieces = [(lo, hi - SIDE), (hi - SIDE, PIX - first)]
                for p_lo, p_hi in pieces:
                    nc.sync.dma_start(out=v_win[p_lo:p_hi, t, o, :], in_=parked[first + p_lo : first + p_hi, :])

        def project_channels_first(part):
            w_codes, w_scales = quantise_weight(part, True)
            projected = sums.tile([P, CH_TILES, PIX], F32, tag="sums", name="projected_" + part)
            for b in range(CH_TILES):
                for g in range(PASSES):
                    nc.tensor.matmul_mx(
                        out=projected[:, b, :],
                        lhsT=w_codes[:, b, g, :].bitcast(FP8X4),
                        lhsT_scale=w_scales[:, b, g, :],
                        rhs=x_codes[:, g, :].bitcast(FP8X4),
                        rhs_scale=x_scales[:, g, :],
                        start=(g == 0),
                        stop=(g == PASSES - 1),
                    )
            return projected[:].rearrange("p b (y x) -> p b y x", x=SIDE)

        nc.scalar.copy(out=k_pad[:, :, PAD : PAD + SIDE, PAD : PAD + SIDE], in_=project_channels_first("k"))
        q_psum = project_channels_first("q")
        q_sb = keep.tile([P, CH_TILES, SIDE, SIDE], F32)
        nc.vector.tensor_copy(out=q_sb[:], in_=q_psum)

        rows_of_softmax = PIX_TILES * HEADS
        scores = keep.tile([P, WIN, rows_of_softmax], F32)
        for o_first in range(0, WIN, 2):
            n = min(2, WIN - o_first)
            halves = stream.tile([P, 2, PIX_TILES, P], F32, tag="stream")
            for oo in range(n):
                i, j = divmod(o_first + oo, KSIZE)
                k_window = k_pad[:, :, i : i + SIDE, j : j + SIDE]
                qk = work.tile([P, CH_TILES, PIX], F32, bufs=8)
                qk_image = qk[:].rearrange("p b (y x) -> p b y x", x=SIDE)
                if oo == 0:
                    nc.vector.tensor_tensor(out=qk_image, in0=q_psum, in1=k_window, op=ALU.mult)
                else:
                    nc.gpsimd.tensor_tensor(out=qk_image, in0=q_sb[:], in1=k_window, op=ALU.mult)
                for t in range(PIX_TILES):
                    for b in range(CH_TILES):
                        nc.tensor.matmul(
                            out=halves[:, oo, t, :],
                            lhsT=qk[:, b, t * P : (t + 1) * P],
                            rhs=ident[:],
                            is_transpose=True,
                            start=(b == 0),
                            stop=(b == CH_TILES - 1),
                        )
            nc.vector.tensor_reduce(
                out=scores[:, o_first : o_first + n, :].rearrange("p o r -> p (o r)"),
                in_=halves[:, 0:n].rearrange("p o t (h c) -> p (o t h) c", c=HALF_HEAD),
                axis=AXIS_X,
                op=ALU.add,
            )

        top = small.tile([P, rows_of_softmax], F32)
        nc.vector.tensor_reduce(out=top[:], in_=scores[:].rearrange("p o r -> p r o"), axis=AXIS_X, op=ALU.max)
        centred = keep.tile([P, WIN, rows_of_softmax], F32)
        nc.vector.tensor_tensor(
            out=centred[:],
            in0=scores[:],
            in1=top[:].unsqueeze(1).to_broadcast([P, WIN, rows_of_softmax]),
            op=ALU.subtract,
        )
        e = keep.tile([P, WIN, rows_of_softmax], F32)
        nc.scalar.activation(out=e[:], in_=centred[:], func=ACT.Exp)
        total = small.tile([P, rows_of_softmax], F32)
        nc.vector.tensor_reduce(out=total[:], in_=e[:].rearrange("p o r -> p r o"), axis=AXIS_X, op=ALU.add)
        inv = small.tile([P, rows_of_softmax], F32)
        nc.vector.reciprocal(out=inv[:], in_=total[:])
        inv_inside = small.tile([P, KSIZE, rows_of_softmax], F32)
        nc.vector.tensor_tensor(
            out=inv_inside[:],
            in0=inv[:].unsqueeze(1).to_broadcast([P, KSIZE, rows_of_softmax]),
            in1=inside[:].unsqueeze(2).to_broadcast([P, KSIZE, rows_of_softmax]),
            op=ALU.mult,
        )
        att = keep.tile([P, WIN, PIX_TILES, HEADS], F32)
        nc.vector.tensor_tensor(
            out=att[:].rearrange("p (i j) t h -> p i (j t h)", j=KSIZE),
            in0=e[:].rearrange("p (i j) r -> p i (j r)", j=KSIZE),
            in1=inv_inside[:].rearrange("p j r -> p (j r)").unsqueeze(1).to_broadcast([P, KSIZE, KSIZE * rows_of_softmax]),
            op=ALU.mult,
        )

        out_view = out.rearrange("n (ct c) h w -> c (n ct) (h w)", ct=CH_TILES, c=P)
        for t in range(PIX_TILES):
            result = [sums.tile([P, P], F32, tag="sums", name="result_%d" % ct) for ct in range(CH_TILES)]
            chunks = [(o, KSIZE) for o in range(0, WIN, KSIZE)]
            if t == PIX_TILES - 1:
                chunks[-1:] = [(WIN - KSIZE, LAST_CUT), (WIN - KSIZE + LAST_CUT, KSIZE - LAST_CUT)]
            for o_first, n in chunks:
                av = work.tile([P, KSIZE, D], F32)
                nc.vector.tensor_tensor(
                    out=av[:, 0:n, :].rearrange("p o (h c) -> p o h c", h=HEADS),
                    in0=v_win[:, t, o_first : o_first + n, :].rearrange("p o (h c) -> p o h c", h=HEADS),
                    in1=att[:, o_first : o_first + n, t, :].unsqueeze(3).to_broadcast([P, n, HEADS, HEAD_DIM]),
                    op=ALU.mult,
                )
                for oo in range(n):
                    for ct in range(CH_TILES):
                        nc.tensor.matmul(
                            out=result[ct][:],
                            lhsT=av[:, oo, ct * P : (ct + 1) * P],
                            rhs=ident[:],
                            is_transpose=True,
                            start=(o_first + oo == 0),
                            stop=(o_first + oo == WIN - 1),
                        )
            out_sb = small.tile([P, CH_TILES, P], F32)
            for ct in range(CH_TILES):
                nc.scalar.copy(out=out_sb[:, ct, :], in_=result[ct][:])
            nc.sync.dma_start(out=out_view[:, :, t * P : (t + 1) * P], in_=out_sb[:])
